import numpy as np
import ml_dtypes


def mxq(x, axis, fmt="e4m3"):
    dtype, down = {"e4m3": (ml_dtypes.float8_e4m3fn, 7), "e5m2": (ml_dtypes.float8_e5m2, 14)}[fmt]
    v = np.moveaxis(np.asarray(x, np.float32).astype(ml_dtypes.bfloat16).astype(np.float64), axis, -1)
    blocks = v.reshape(v.shape[:-1] + (-1, 32))
    amax = np.abs(blocks).max(-1, keepdims=True)
    byte = np.maximum(np.where(amax > 0, np.frexp(amax)[1] - 1 + 127, 0) - down, 1)
    scale = np.exp2(byte - 127.0)
    codes = (blocks / scale).astype(np.float32).astype(dtype).astype(np.float64)
    return np.moveaxis((codes * scale).reshape(v.shape), -1, axis)


WIDE = False


def mx_kscale(k):
    if not WIDE:
        return np.ones(k)
    levels = np.array([10, -10, 5, -5, 0])
    if k % 512:
        return np.exp2(np.random.permutation(np.resize(levels, k // 32))).repeat(32)
    a = np.empty((k // 512, 16))
    for p in range(k // 512):
        a[p, :8] = np.random.permutation(np.resize(levels, 8))
        for g in range(8):
            far = levels[np.abs(levels - a[p, g]) >= 10]
            a[p, g + 8] = far[np.random.randint(len(far))]
    return np.exp2(a.ravel()).repeat(32)


BF16 = ml_dtypes.bfloat16


def bf(x):
    return np.asarray(x, np.float32).astype(BF16)


def f64(x):
    return np.asarray(x).astype(np.float64)


N, MUL0, MUL1, MUL2, DIM1, DIM2 = 1024, 768, 128, 128, 3, 5
D_S = MUL0
D_V = MUL1 * DIM1
D_T = MUL2 * DIM2
N_GATES = MUL1 + MUL2
J = MUL0 + N_GATES


def sigmoid(v):
    return 1.0 / (1.0 + np.exp(-v))


def leaky_relu(v):
    return np.where(v >= 0.0, v, 0.01 * v)


def linear_parts(x, W0, W1, W2):
    x = f64(x)
    n = x.shape[0]
    s = x[:, :D_S]
    v = x[:, D_S:D_S + D_V].reshape(n, MUL1, DIM1)
    t = x[:, D_S + D_V:].reshape(n, MUL2, DIM2)
    s_out = (s @ f64(W0)) / np.sqrt(MUL0)
    v_out = (v.transpose(0, 2, 1) @ f64(W1)).transpose(0, 2, 1) / np.sqrt(MUL1)
    t_out = (t.transpose(0, 2, 1) @ f64(W2)).transpose(0, 2, 1) / np.sqrt(MUL2)
    return s_out, v_out, t_out


def setup_inputs():
    s = mx_kscale(N)[:, None]
    u = mx_kscale(J)
    uv = u[MUL0:MUL0 + MUL1]
    ut = u[MUL0 + MUL1:]
    ug = np.concatenate([u[:MUL0], np.repeat(uv, DIM1), np.repeat(ut, DIM2)])
    x0 = bf(np.random.standard_normal((N, D_S + D_V + D_T)))
    W0_0 = bf(np.random.standard_normal((MUL0, J)))
    W1_0 = bf(np.random.standard_normal((MUL1, MUL1)))
    W2_0 = bf(np.random.standard_normal((MUL2, MUL2)))
    g = bf(np.random.standard_normal((N, D_S + D_V + D_T)) * np.exp2(np.random.randint(-6, 1, (N, 1))) * 4.0 / s * ug)
    s_out, v_out, t_out = linear_parts(x0, W0_0, W1_0, W2_0)
    xs = f64(x0).copy()
    xs[:, :D_S] = xs[:, :D_S] * s
    return {"x": bf(xs), "W0": bf(f64(W0_0) / u[None, :]), "W1": bf(f64(W1_0) / uv[None, :]), "W2": bf(f64(W2_0) / ut[None, :]),
            "s_out": np.asarray(s_out, np.float32), "v_out": np.asarray(v_out, np.float32),
            "t_out": np.asarray(t_out, np.float32), "grad_out": g}


def reference(x, W0, W1, W2, s_out, v_out, t_out, grad_out):
    g = f64(grad_out)
    n = g.shape[0]
    z = f64(s_out)
    g_s = g[:, :D_S]
    g_v = g[:, D_S:D_S + D_V].reshape(n, MUL1, DIM1)
    g_t = g[:, D_S + D_V:].reshape(n, MUL2, DIM2)
    d_scal = g_s * np.where(z[:, :MUL0] >= 0.0, 1.0, 0.01)
    gates = sigmoid(z[:, MUL0:])
    d_gates = np.concatenate([(g_v * f64(v_out)).sum(axis=2), (g_t * f64(t_out)).sum(axis=2)], axis=1)
    dz = np.concatenate([d_scal, d_gates * gates * (1.0 - gates)], axis=1)
    s = f64(x)[:, :D_S]
    ds = (mxq(dz, 1, "e5m2") @ mxq(f64(W0), 1, "e4m3").T) / np.sqrt(MUL0)
    dW0 = (mxq(s, 0, "e4m3").T @ mxq(dz, 0, "e5m2")) / np.sqrt(MUL0)
    hv = g_v * gates[:, :MUL1, None]
    ht = g_t * gates[:, MUL1:, None]
    dv = (hv.transpose(0, 2, 1) @ f64(W1).T).transpose(0, 2, 1) / np.sqrt(MUL1)
    dt = (ht.transpose(0, 2, 1) @ f64(W2).T).transpose(0, 2, 1) / np.sqrt(MUL2)
    dx = np.concatenate([ds, dv.reshape(n, -1), dt.reshape(n, -1)], axis=1)
    return dx, dW0

@@ -1,0 +1,403 @@
+from contextlib import ExitStack
+import math
+
+import concourse.masks as masks
+import concourse.mybir as mybir
+
+FLOPS = 2 * 2 * 1024 * 1024 * 768 + 2 * 1024 * 8 * 128 * 128
+BYTES = 25755648
+
+F32 = mybir.dt.float32
+BF16 = mybir.dt.bfloat16
+U32 = mybir.dt.uint32
+U8 = mybir.dt.uint8
+E4 = mybir.dt.float8_e4m3fn_x4
+E5 = mybir.dt.float8_e5m2_x4
+ALU = mybir.AluOpType
+ACT = mybir.ActivationFunctionType
+AX = mybir.AxisListType
+
+P = 128
+C768 = 1.0 / math.sqrt(768.0)
+C128 = 1.0 / math.sqrt(128.0)
+
+
+def tile_equivariantmlpblock_v_kernel(tc, x, W0, W1, W2, s_out, v_out, t_out, grad_out, out_0, out_1):
+    nc = tc.nc
+
+    go_v = grad_out.rearrange("(g p j) w -> p g j w", g=2, j=4)
+    z_v = s_out.rearrange("(g p j) w -> p g j w", g=2, j=4)
+    v_v = v_out.rearrange("(g p j) o m -> p g j (o m)", g=2, j=4)
+    t_v = t_out.rearrange("(g p j) o m -> p g j (o m)", g=2, j=4)
+    x_v = x.rearrange("(g p j) w -> p g j w", g=2, j=4)
+    w0_v = W0.rearrange("(t p) f -> p t f", p=P)
+    o0_v = out_0.rearrange("(g p j) w -> p g j w", g=2, j=4)
+    o1_v = out_1.rearrange("(t p) f -> p t f", p=P)
+
+    with ExitStack() as ctx:
+        const = ctx.enter_context(tc.tile_pool(name="const", bufs=1))
+        inp = ctx.enter_context(tc.tile_pool(name="inp", bufs=1))
+        work = ctx.enter_context(tc.tile_pool(name="work", bufs=2))
+        psum = ctx.enter_context(tc.psum_pool(name="psum", bufs=1))
+        ctx.enter_context(tc.manual_schedule())
+
+        ident_f = const.tile([P, P], F32, name="ident_f")
+        masks.make_identity(nc, ident_f[:])
+        ident_b = const.tile([P, P], BF16, name="ident_b")
+        masks.make_identity(nc, ident_b[:])
+        neg_half = const.tile([P, 1], F32, name="neg_half")
+        nc.vector.memset(neg_half[:], -0.5)
+        warm = const.tile([P, 1], F32, name="warm")
+        nc.scalar.activation(out=warm[:], in_=neg_half[:], func=ACT.Sigmoid)
+
+        w1_raw = inp.tile([P, P], BF16, name="w1_raw")
+        nc.sync.dma_start(out=w1_raw[:], in_=W1)
+        w2_raw = inp.tile([P, P], BF16, name="w2_raw")
+        nc.sync.dma_start(out=w2_raw[:], in_=W2)
+        x_raw = []
+        for g in range(2):
+            xr = inp.tile([P, 4, 768], BF16, name="x_raw%d" % g)
+            nc.sync.dma_start(out=xr[:], in_=x_v[:, g, :, 0:768])
+            x_raw.append(xr)
+        go_u = []
+        z_u = []
+        v_u = []
+        t_u = []
+        for U in range(4):
+            go_u.append(inp.tile([P, 2, 1792], BF16, name="go%d" % U))
+            z_u.append(inp.tile([P, 2, 1024], F32, name="z%d" % U))
+            v_u.append(inp.tile([P, 2, 384], F32, name="v%d" % U))
+            t_u.append(inp.tile([P, 2, 640], F32, name="t%d" % U))
+
+        def load_rows(U, e0, e1):
+            g = U // 2
+            j0 = 2 * (U % 2)
+            nc.sync.dma_start(out=go_u[U][:, e0:e1, :], in_=go_v[:, g, j0 + e0:j0 + e1, :])
+            nc.sync.dma_start(out=z_u[U][:, e0:e1, :], in_=z_v[:, g, j0 + e0:j0 + e1, :])
+            nc.sync.dma_start(out=v_u[U][:, e0:e1, :], in_=v_v[:, g, j0 + e0:j0 + e1, :])
+            nc.sync.dma_start(out=t_u[U][:, e0:e1, :], in_=t_v[:, g, j0 + e0:j0 + e1, :])
+
+        w0_raw = inp.tile([P, 6, 1024], BF16, name="w0_raw")
+        for c in range(3):
+            nc.sync.dma_start(out=w0_raw[:, 2 * c:2 * c + 2, :], in_=w0_v[:, 2 * c:2 * c + 2, :])
+        load_rows(0, 0, 1)
+        load_rows(0, 1, 2)
+        load_rows(1, 0, 2)
+        load_rows(2, 0, 2)
+        load_rows(3, 0, 2)
+
+        w0c = const.tile([P, 2, 768], U32, name="w0c", align_bytes=64)
+        w0s = const.tile([P, 2, 768], U8, name="w0s", align_bytes=64)
+        xc = const.tile([P, 2, 768], U32, name="xc", align_bytes=64)
+        xs = const.tile([P, 2, 768], U8, name="xs", align_bytes=64)
+        dkc = const.tile([P, 2, 1024], U32, name="dkc", align_bytes=64)
+        dks = const.tile([P, 2, 1024], U8, name="dks", align_bytes=64)
+        dzn = const.tile([P, 8, 1024], BF16, name="dzn", align_bytes=64)
+        w1T = const.tile([P, P], F32, name="w1T")
+        w2T = const.tile([P, P], F32, name="w2T")
+
+        def evac(eng, out, in_, scale):
+            if eng == 0:
+                nc.scalar.activation(out=out, in_=in_, func=ACT.Copy, scale=scale)
+            else:
+                nc.vector.tensor_scalar(out=out, in0=in_, scalar1=scale, scalar2=None, op0=ALU.mult)
+
+        xg_t = {}
+
+        def x_copy(k):
+            g = k // 3
+            c = k % 3
+            xg = work.tile([P, 256, 4], BF16, name="xg", tag="dk", bufs=4, align_bytes=64)
+            nc.vector.tensor_copy(out=xg[:], in_=x_raw[g][:, :, 256 * c:256 * (c + 1)].rearrange("p j i -> p i j"))
+            xg_t[k] = xg
+
+        def x_quant(k):
+            g = k // 3
+            c = k % 3
+            nc.vector.quantize_mx(out=xc[:, g, 256 * c:256 * (c + 1)].bitcast(E4),
+                                  scales=xs[:, g, 256 * c:256 * (c + 1)],
+                                  in_=xg_t[k][:].rearrange("p i j -> p (i j)"))
+
+        w0g_t = {}
+        W0_BANKS = ("pA", "pB", "pm0", "pm1", "pd", "pz")
+
+        def w0_turn(c):
+            w0g = work.tile([P, 2, 256, 4], BF16, name="w0g", tag="o0", bufs=3, align_bytes=64)
+            w0g_t[c] = w0g
+            for s in range(2):
+                words = w0_raw[:, 2 * c + s, :].bitcast(F32)
+                pt = psum.tile([P, 2, 2, P], F32, name="pt", tag=W0_BANKS[2 * c + s])
+                for G in range(2):
+                    for u in range(2):
+                        nc.tensor.transpose(pt[:, G, u, :], words[:, 256 * G + u:256 * (G + 1):2], ident_f[:])
+                for G in range(2):
+                    nc.scalar.copy(out=w0g[:, G, P * s:P * (s + 1), :].bitcast(F32),
+                                   in_=pt[:, G, :, :].rearrange("p u r -> p r u"))
+
+        def w0_quant(c):
+            for G in range(2):
+                nc.vector.quantize_mx(out=w0c[:, G, 256 * c:256 * (c + 1)].bitcast(E4),
+                                      scales=w0s[:, G, 256 * c:256 * (c + 1)],
+                                      in_=w0g_t[c][:, G, :, :].rearrange("p i t -> p (i t)"))
+
+        pz_t = {}
+        pg_t = {}
+        gT_t = {}
+        hT_t = {}
+        o0_t = {}
+        q_t = {}
+        dg_t = {}
+        pv_t = {}
+        pd_t = {}
+        dTg_t = {}
+        dT_t = {}
+        pm_t = {}
+
+        def p1(s):
+            go = go_u[s // 2]
+            z = z_u[s // 2]
+            e = s % 2
+            pz = psum.tile([P, 2, P], F32, name="pz", tag="pz")
+            for k in range(2):
+                nc.tensor.transpose(pz[:, k, :], z[:, e, 768 + P * k:768 + P * (k + 1)], ident_f[:])
+            pg = psum.tile([P, 8, P], BF16, name="pg", tag="pg", bufs=2)
+            for m in range(3):
+                nc.tensor.transpose(pg[:, m, :], go[:, e, 768 + m:1152:3], ident_b[:])
+            for m in range(5):
+                nc.tensor.transpose(pg[:, 3 + m, :], go[:, e, 1152 + m:1792:5], ident_b[:])
+            pz_t[s] = pz
+            pg_t[s] = pg
+
+        def s1(s):
+            gT = work.tile([P, 2, P], F32, name="gT", tag="gT")
+            nc.scalar.activation(out=gT[:], in_=pz_t[s][:], func=ACT.Sigmoid)
+            gT_t[s] = gT
+
+        def s2(s):
+            q = work.tile([P, 256], F32, name="q", tag="q")
+            nc.scalar.activation(out=q[:], in_=z_u[s // 2][:, s % 2, 768:1024], func=ACT.Sigmoid)
+            nc.scalar.activation(out=q[:], in_=q[:], func=ACT.Square, bias=neg_half[:])
+            q_t[s] = q
+
+        def v_mask(s):
+            zs = z_u[s // 2][:, s % 2, 0:768]
+            nc.vector.tensor_scalar(out=zs, in0=zs, scalar1=0.0, scalar2=0.01, op0=ALU.is_ge, op1=ALU.max)
+
+        def v_dzs(s):
+            nc.vector.tensor_tensor(out=dzn[:, s, 0:768], in0=go_u[s // 2][:, s % 2, 0:768],
+                                    in1=z_u[s // 2][:, s % 2, 0:768], op=ALU.mult)
+
+        def v_hv(s):
+            hT = work.tile([P, 8, P], F32, name="hT", tag="hT")
+            hT_t[s] = hT
+            nc.vector.tensor_tensor(out=hT[:, 0:3, :], in0=pg_t[s][:, 0:3, :],
+                                    in1=gT_t[s][:, 0:1, :].to_broadcast([P, 3, P]), op=ALU.mult)
+
+        def v_ht(s):
+            nc.vector.tensor_tensor(out=hT_t[s][:, 3:8, :], in0=pg_t[s][:, 3:8, :],
+                                    in1=gT_t[s][:, 1:2, :].to_broadcast([P, 5, P]), op=ALU.mult)
+
+        def v_prodv(s):
+            vv = v_u[s // 2][:, s % 2, :]
+            nc.vector.scalar_tensor_tensor(out=vv, in0=go_u[s // 2][:, s % 2, 768:1152], scalar=-1.0, in1=vv,
+                                           op0=ALU.mult, op1=ALU.mult)
+
+        def v_prodt(s):
+            tt = t_u[s // 2][:, s % 2, :]
+            nc.vector.scalar_tensor_tensor(out=tt, in0=go_u[s // 2][:, s % 2, 1152:1792], scalar=-1.0, in1=tt,
+                                           op0=ALU.mult, op1=ALU.mult)
+
+        def v_redv(s):
+            dg = work.tile([P, 256], F32, name="dg", tag="dg")
+            dg_t[s] = dg
+            nc.vector.tensor_reduce(out=dg[:, 0:128], in_=v_u[s // 2][:, s % 2, :].rearrange("p (o m) -> p o m", m=3),
+                                    axis=AX.X, op=ALU.add)
+
+        def v_redt(s):
+            nc.vector.tensor_reduce(out=dg_t[s][:, 128:256],
+                                    in_=t_u[s // 2][:, s % 2, :].rearrange("p (o m) -> p o m", m=5),
+                                    axis=AX.X, op=ALU.add)
+
+        def v_dzg(s):
+            nc.vector.scalar_tensor_tensor(out=dzn[:, s, 768:1024], in0=q_t[s][:], scalar=0.25,
+                                           in1=dg_t[s][:], op0=ALU.subtract, op1=ALU.mult)
+
+        def p2(s):
+            pB = psum.tile([P, 4, P], F32, name="pB", tag="pB")
+            for m in range(3):
+                nc.tensor.matmul(pB[:, m, :], lhsT=hT_t[s][:, m, :], rhs=w1T[:], start=True, stop=True)
+            nc.tensor.matmul(pB[:, 3, :], lhsT=hT_t[s][:, 7, :], rhs=w2T[:], start=True, stop=True)
+            pA = psum.tile([P, 4, P], F32, name="pA", tag="pA")
+            for m in range(4):
+                nc.tensor.matmul(pA[:, m, :], lhsT=hT_t[s][:, 3 + m, :], rhs=w2T[:], start=True, stop=True)
+            pv_t[s] = (pA, pB)
+
+        def s3v(s):
+            o0 = work.tile([P, 1792], F32, name="o0", tag="o0", bufs=3, align_bytes=64)
+            o0_t[s] = o0
+            pB = pv_t[s][1]
+            evac(0, o0[:, 768:1152].rearrange("p (i m) -> p i m", m=3), pB[:, 0:3, :].rearrange("p m i -> p i m"), C128)
+            evac(0, o0[:, 1152:1792].rearrange("p (i m) -> p i m", m=5)[:, :, 4], pB[:, 3, :], C128)
+
+        def s3t(s):
+            evac(0, o0_t[s][:, 1152:1792].rearrange("p (i m) -> p i m", m=5)[:, :, 0:4],
+                 pv_t[s][0][:].rearrange("p m i -> p i m"), C128)
+
+        def p3(s):
+            words = dzn[:, s, :].bitcast(F32)
+            pd = psum.tile([P, 2, 2, P], F32, name="pd", tag="pd")
+            for G in range(2):
+                for u in range(2):
+                    nc.tensor.transpose(pd[:, G, u, :], words[:, 256 * G + u:256 * (G + 1):2], ident_f[:])
+            pd_t[s] = pd
+
+        def s4(s):
+            dTg = work.tile([P, 2, P, 4], BF16, name="dTg", tag="dTg", align_bytes=64)
+            for G in range(2):
+                nc.scalar.copy(out=dTg[:, G, :, :].bitcast(F32), in_=pd_t[s][:, G, :, :].rearrange("p u r -> p r u"))
+            dTg_t[s] = dTg
+
+        def v3(s):
+            dTc = work.tile([P, 256], U32, name="dTc", tag="dTc", align_bytes=64)
+            dTs = work.tile([P, 256], U8, name="dTs", tag="dTs", align_bytes=64)
+            nc.vector.quantize_mx(out=dTc[:].bitcast(E5), scales=dTs[:],
+                                  in_=dTg_t[s][:].rearrange("p g r t -> p (g r t)"))
+            dT_t[s] = (dTc, dTs)
+
+        def p4(s):
+            dTc, dTs = dT_t[s]
+            pms = []
+            for w in range(2):
+                pm = psum.tile([P, 512], F32, name="pm", tag="pm%d" % w)
+                for G in range(2):
+                    nc.tensor.matmul_mx(out=pm[:],
+                                        lhsT=dTc[:, P * G:P * (G + 1)].bitcast(E5),
+                                        lhsT_scale=dTs[:, P * G:P * (G + 1)],
+                                        rhs=w0c[:, G, 256 * w:256 * w + 512].bitcast(E4),
+                                        rhs_scale=w0s[:, G, 256 * w:256 * w + 512],
+                                        start=(G == 0), stop=(G == 1))
+                pms.append(pm)
+            pm_t[s] = pms
+
+        def s5(s, eng1):
+            o0 = o0_t[s]
+            evac(0, o0[:, 0:512], pm_t[s][0][:], C768)
+            evac(eng1, o0[:, 512:768], pm_t[s][1][:, 256:512], C768)
+            nc.sync.dma_start(out=o0_v[:, s // 4, s % 4, :], in_=o0[:])
+
+        dk_t = {}
+
+        def tok_copy(g, c, eng):
+            dk = work.tile([P, 256, 4], BF16, name="dk", tag="dk", bufs=4, align_bytes=64)
+            src = dzn[:, 4 * g:4 * g + 4, 256 * c:256 * (c + 1)].rearrange("p j f -> p f j")
+            if eng == 0:
+                nc.scalar.copy(out=dk[:], in_=src)
+            else:
+                nc.vector.tensor_copy(out=dk[:], in_=src)
+            dk_t[(g, c)] = dk
+
+        def tok_quant(g, c):
+            nc.vector.quantize_mx(out=dkc[:, g, 256 * c:256 * (c + 1)].bitcast(E5),
+                                  scales=dks[:, g, 256 * c:256 * (c + 1)],
+                                  in_=dk_t[(g, c)][:].rearrange("p f j -> p (f j)"))
+
+        grp_t = {}
+
+        def dw_pass(it, h, g, bank):
+            if g == 0:
+                grp_t[(it, h)] = psum.tile([P, 512], F32, name="pw", tag=bank, bufs=(2 if bank == "pg" else 1))
+            nc.tensor.matmul_mx(out=grp_t[(it, h)][:],
+                                lhsT=xc[:, g, P * it:P * (it + 1)].bitcast(E4),
+                                lhsT_scale=xs[:, g, P * it:P * (it + 1)],
+                                rhs=dkc[:, g, 512 * h:512 * (h + 1)].bitcast(E5),
+                                rhs_scale=dks[:, g, 512 * h:512 * (h + 1)],
+                                start=(g == 0), stop=(g == 1))
+
+        def dw_out(it0, h):
+            o1 = work.tile([P, 2, 512], F32, name="o1", tag="o1", bufs=3)
+            evac(1, o1[:, 0, :], grp_t[(it0, h)][:], C768)
+            evac(0, o1[:, 1, :], grp_t[(it0 + 1, h)][:], C768)
+            nc.sync.dma_start(out=o1_v[:, it0:it0 + 2, 512 * h:512 * (h + 1)], in_=o1[:])
+
+        for (raw, dst, bank) in ((w1_raw, w1T, "pg"), (w2_raw, w2T, "pz")):
+            pw = psum.tile([P, P], BF16, name="pw12", tag=bank, bufs=(2 if bank == "pg" else 1))
+            nc.tensor.transpose(pw[:], raw[:], ident_b[:])
+            nc.scalar.copy(out=dst[:], in_=pw[:])
+        for c in range(3):
+            w0_turn(c)
+        x_copy(0)
+        x_copy(1)
+        for k in range(2, 6):
+            x_quant(k - 2)
+            x_copy(k)
+        x_quant(4)
+        x_quant(5)
+        for c in range(3):
+            w0_quant(c)
+        p1(0)
+        s1(0)
+
+        early = ("pz", "pg", "pg")
+        late = ("pB", "pA", "pd")
+        for s in range(8):
+            v_mask(s)
+            if s >= 1:
+                v_dzg(s - 1)
+                p3(s - 1)
+            v_hv(s)
+            v_ht(s)
+            if s >= 1:
+                s4(s - 1)
+            if s < 7:
+                p1(s + 1)
+                s1(s + 1)
+            else:
+                for it in range(3):
+                    dw_pass(it, 0, 0, early[it])
+            s2(s)
+            p2(s)
+            v_prodv(s)
+            v_dzs(s)
+            if s >= 1:
+                v3(s - 1)
+            if s >= 5:
+                tok_quant(0, s - 5)
+            s3v(s)
+            s3t(s)
+            if s >= 1:
+                p4(s - 1)
+            v_prodt(s)
+            v_redv(s)
+            v_redt(s)
+            if s >= 1:
+                s5(s - 1, 0)
+            if s >= 4:
+                tok_copy(0, s - 4, 0)
+
+        tok_quant(0, 3)
+        v_dzg(7)
+        p3(7)
+        tok_copy(1, 0, 1)
+        tok_copy(1, 1, 1)
+        s4(7)
+        tok_copy(1, 3, 0)
+        for it in range(3, 6):
+            dw_pass(it, 0, 0, late[it - 3])
+        tok_quant(1, 0)
+        tok_quant(1, 1)
+        tok_copy(1, 2, 1)
+        v3(7)
+        tok_quant(1, 2)
+        tok_quant(1, 3)
+        for it in range(6):
+            dw_pass(it, 0, 1, "")
+            if it % 2 == 1:
+                dw_out(it - 1, 0)
+        p4(7)
+        s5(7, 1)
+        banks1 = early + late
+        for it in range(6):
+            dw_pass(it, 1, 0, banks1[it])
+            dw_pass(it, 1, 1, "")
+            if it % 2 == 1:
+                dw_out(it - 1, 1)

@@ -84,7 +84,6 @@ def tile_equivariantmlpblock_v_kernel(tc, x, W0, W1, W2, s_out, v_out, t_out, gr
         load_rows(0, 1, 2)
         load_rows(1, 0, 2)
         load_rows(2, 0, 2)
-        load_rows(3, 0, 2)
 
         w0c = const.tile([P, 2, 768], U32, name="w0c", align_bytes=64)
         w0s = const.tile([P, 2, 768], U8, name="w0s", align_bytes=64)
@@ -122,7 +121,7 @@ def tile_equivariantmlpblock_v_kernel(tc, x, W0, W1, W2, s_out, v_out, t_out, gr
         W0_BANKS = ("pA", "pB", "pm0", "pm1", "pd", "pz")
 
         def w0_turn(c):
-            w0g = work.tile([P, 2, 256, 4], BF16, name="w0g", tag="o0", bufs=3, align_bytes=64)
+            w0g = work.tile([P, 2, 256, 4], BF16, name="w0g", tag="o0", bufs=4, align_bytes=64)
             w0g_t[c] = w0g
             for s in range(2):
                 words = w0_raw[:, 2 * c + s, :].bitcast(F32)
@@ -233,7 +232,7 @@ def tile_equivariantmlpblock_v_kernel(tc, x, W0, W1, W2, s_out, v_out, t_out, gr
             pv_t[s] = (pA, pB)
 
         def s3v(s):
-            o0 = work.tile([P, 1792], F32, name="o0", tag="o0", bufs=3, align_bytes=64)
+            o0 = work.tile([P, 1792], F32, name="o0", tag="o0", bufs=4, align_bytes=64)
             o0_t[s] = o0
             pB = pv_t[s][1]
             evac(0, o0[:, 768:1152].rearrange("p (i m) -> p i m", m=3), pB[:, 0:3, :].rearrange("p m i -> p i m"), C128)
@@ -371,28 +370,34 @@ def tile_equivariantmlpblock_v_kernel(tc, x, W0, W1, W2, s_out, v_out, t_out, gr
             v_redt(s)
             if s >= 1:
                 s5(s - 1, 0)
-            if s >= 4:
+            if s == 1 or s == 2:
+                load_rows(3, s - 1, s)
+            if 4 <= s <= 6:
                 tok_copy(0, s - 4, 0)
 
-        tok_quant(0, 3)
         v_dzg(7)
         p3(7)
         tok_copy(1, 0, 1)
         tok_copy(1, 1, 1)
         s4(7)
         tok_copy(1, 3, 0)
-        for it in range(3, 6):
-            dw_pass(it, 0, 0, late[it - 3])
+        dw_pass(3, 0, 0, "pB")
+        dw_pass(4, 0, 0, "pA")
         tok_quant(1, 0)
         tok_quant(1, 1)
         tok_copy(1, 2, 1)
+        tok_copy(0, 3, 1)
         v3(7)
-        tok_quant(1, 2)
-        tok_quant(1, 3)
-        for it in range(6):
+        for it in range(5):
             dw_pass(it, 0, 1, "")
-            if it % 2 == 1:
-                dw_out(it - 1, 0)
+        dw_pass(5, 0, 0, "pd")
+        dw_pass(5, 0, 1, "")
+        dw_out(0, 0)
+        tok_quant(1, 2)
+        tok_quant(0, 3)
+        tok_quant(1, 3)
+        dw_out(2, 0)
+        dw_out(4, 0)
         p4(7)
         s5(7, 1)
         banks1 = early + late

@@ -144,6 +144,7 @@ def tile_equivariantmlpblock_v_kernel(tc, x, W0, W1, W2, s_out, v_out, t_out, gr
         gT_t = {}
         hT_t = {}
         o0_t = {}
+        tS_t = {}
         q_t = {}
         dg_t = {}
         pv_t = {}
@@ -234,13 +235,18 @@ def tile_equivariantmlpblock_v_kernel(tc, x, W0, W1, W2, s_out, v_out, t_out, gr
         def s3v(s):
             o0 = work.tile([P, 1792], F32, name="o0", tag="o0", bufs=4, align_bytes=64)
             o0_t[s] = o0
+            tS = work.tile([P, 5, P], F32, name="tS", tag="tS")
+            tS_t[s] = tS
             pB = pv_t[s][1]
             evac(0, o0[:, 768:1152].rearrange("p (i m) -> p i m", m=3), pB[:, 0:3, :].rearrange("p m i -> p i m"), C128)
-            evac(0, o0[:, 1152:1792].rearrange("p (i m) -> p i m", m=5)[:, :, 4], pB[:, 3, :], C128)
+            evac(0, tS[:, 4, :], pB[:, 3, :], C128)
 
         def s3t(s):
-            evac(0, o0_t[s][:, 1152:1792].rearrange("p (i m) -> p i m", m=5)[:, :, 0:4],
-                 pv_t[s][0][:].rearrange("p m i -> p i m"), C128)
+            tS = tS_t[s]
+            evac(0, tS[:, 0:4, :], pv_t[s][0][:], C128)
+            nc.gpsimd.tensor_scalar(out=o0_t[s][:, 1152:1792].rearrange("p (i m) -> p i m", m=5),
+                                    in0=tS[:].rearrange("p m i -> p i m"),
+                                    scalar1=1.0, scalar2=0.0, op0=ALU.mult, op1=ALU.add)
 
         def p3(s):
             words = dzn[:, s, :].bitcast(F32)
@@ -357,16 +363,15 @@ def tile_equivariantmlpblock_v_kernel(tc, x, W0, W1, W2, s_out, v_out, t_out, gr
             p2(s)
             v_prodv(s)
             v_dzs(s)
-            if s >= 1:
-                v3(s - 1)
-            if s >= 5:
-                tok_quant(0, s - 5)
             s3v(s)
             s3t(s)
-            if s >= 1:
-                p4(s - 1)
             v_prodt(s)
             v_redv(s)
+            if s >= 1:
+                v3(s - 1)
+                p4(s - 1)
+            if s >= 5:
+                tok_quant(0, s - 5)
             v_redt(s)
             if s >= 1:
                 s5(s - 1, 0)

@@ -56,9 +56,7 @@ def tile_equivariantmlpblock_v_kernel(tc, x, W0, W1, W2, s_out, v_out, t_out, gr
         nc.sync.dma_start(out=w2_raw[:], in_=W2)
         x_raw = []
         for g in range(2):
-            xr = inp.tile([P, 4, 768], BF16, name="x_raw%d" % g)
-            nc.sync.dma_start(out=xr[:], in_=x_v[:, g, :, 0:768])
-            x_raw.append(xr)
+            x_raw.append(inp.tile([P, 4, 768], BF16, name="x_raw%d" % g))
         go_u = []
         z_u = []
         v_u = []
@@ -68,22 +66,30 @@ def tile_equivariantmlpblock_v_kernel(tc, x, W0, W1, W2, s_out, v_out, t_out, gr
             z_u.append(inp.tile([P, 2, 1024], F32, name="z%d" % U))
             v_u.append(inp.tile([P, 2, 384], F32, name="v%d" % U))
             t_u.append(inp.tile([P, 2, 640], F32, name="t%d" % U))
-
-        def load_rows(U, e0, e1):
-            g = U // 2
-            j0 = 2 * (U % 2)
-            nc.sync.dma_start(out=go_u[U][:, e0:e1, :], in_=go_v[:, g, j0 + e0:j0 + e1, :])
-            nc.sync.dma_start(out=z_u[U][:, e0:e1, :], in_=z_v[:, g, j0 + e0:j0 + e1, :])
-            nc.sync.dma_start(out=v_u[U][:, e0:e1, :], in_=v_v[:, g, j0 + e0:j0 + e1, :])
-            nc.sync.dma_start(out=t_u[U][:, e0:e1, :], in_=t_v[:, g, j0 + e0:j0 + e1, :])
-
         w0_raw = inp.tile([P, 6, 1024], BF16, name="w0_raw")
+
+        def load_x(g):
+            nc.sync.dma_start(out=x_raw[g][:], in_=x_v[:, g, :, 0:768])
+
+        def load_gz(s):
+            nc.sync.dma_start(out=go_u[s // 2][:, s % 2, :], in_=go_v[:, s // 4, s % 4, :])
+            nc.sync.dma_start(out=z_u[s // 2][:, s % 2, :], in_=z_v[:, s // 4, s % 4, :])
+
+        def load_vt(s):
+            nc.sync.dma_start(out=v_u[s // 2][:, s % 2, :], in_=v_v[:, s // 4, s % 4, :])
+            nc.sync.dma_start(out=t_u[s // 2][:, s % 2, :], in_=t_v[:, s // 4, s % 4, :])
+
+        load_gz(0)
+        load_vt(0)
+        load_gz(1)
         for c in range(3):
             nc.sync.dma_start(out=w0_raw[:, 2 * c:2 * c + 2, :], in_=w0_v[:, 2 * c:2 * c + 2, :])
-        load_rows(0, 0, 1)
-        load_rows(0, 1, 2)
-        load_rows(1, 0, 2)
-        load_rows(2, 0, 2)
+        load_vt(1)
+        for s in range(2, 6):
+            load_gz(s)
+            load_vt(s)
+            if s % 2 == 0:
+                load_x(s // 2 - 1)
 
         w0c = const.tile([P, 2, 768], U32, name="w0c", align_bytes=64)
         w0s = const.tile([P, 2, 768], U8, name="w0s", align_bytes=64)
@@ -107,7 +113,7 @@ def tile_equivariantmlpblock_v_kernel(tc, x, W0, W1, W2, s_out, v_out, t_out, gr
             g = k // 3
             c = k % 3
             xg = work.tile([P, 256, 4], BF16, name="xg", tag="dk", bufs=4, align_bytes=64)
-            nc.vector.tensor_copy(out=xg[:], in_=x_raw[g][:, :, 256 * c:256 * (c + 1)].rearrange("p j i -> p i j"))
+            nc.scalar.copy(out=xg[:], in_=x_raw[g][:, :, 256 * c:256 * (c + 1)].rearrange("p j i -> p i j"))
             xg_t[k] = xg
 
         def x_quant(k):
@@ -118,14 +124,15 @@ def tile_equivariantmlpblock_v_kernel(tc, x, W0, W1, W2, s_out, v_out, t_out, gr
                                   in_=xg_t[k][:].rearrange("p i j -> p (i j)"))
 
         w0g_t = {}
-        W0_BANKS = ("pA", "pB", "pm0", "pm1", "pd", "pz")
+        W0_BANKS = (("pm0", "pm1"), ("pd", "pm0"), ("pm1", "pd"))
+        for c in range(3):
+            w0g_t[c] = work.tile([P, 2, 256, 4], BF16, name="w0g%d" % c, tag="o1", bufs=3, align_bytes=64)
 
         def w0_turn(c):
-            w0g = work.tile([P, 2, 256, 4], BF16, name="w0g", tag="o0", bufs=4, align_bytes=64)
-            w0g_t[c] = w0g
+            w0g = w0g_t[c]
             for s in range(2):
                 words = w0_raw[:, 2 * c + s, :].bitcast(F32)
-                pt = psum.tile([P, 2, 2, P], F32, name="pt", tag=W0_BANKS[2 * c + s])
+                pt = psum.tile([P, 2, 2, P], F32, name="pt", tag=W0_BANKS[c][s])
                 for G in range(2):
                     for u in range(2):
                         nc.tensor.transpose(pt[:, G, u, :], words[:, 256 * G + u:256 * (G + 1):2], ident_f[:])
@@ -147,6 +154,7 @@ def tile_equivariantmlpblock_v_kernel(tc, x, W0, W1, W2, s_out, v_out, t_out, gr
         tS_t = {}
         q_t = {}
         dg_t = {}
+        bc_t = {}
         pv_t = {}
         pd_t = {}
         dTg_t = {}
@@ -207,16 +215,28 @@ def tile_equivariantmlpblock_v_kernel(tc, x, W0, W1, W2, s_out, v_out, t_out, gr
             nc.vector.scalar_tensor_tensor(out=tt, in0=go_u[s // 2][:, s % 2, 1152:1792], scalar=-1.0, in1=tt,
                                            op0=ALU.mult, op1=ALU.mult)
 
-        def v_redv(s):
+        def v_sum_a(s):
             dg = work.tile([P, 256], F32, name="dg", tag="dg")
             dg_t[s] = dg
-            nc.vector.tensor_reduce(out=dg[:, 0:128], in_=v_u[s // 2][:, s % 2, :].rearrange("p (o m) -> p o m", m=3),
-                                    axis=AX.X, op=ALU.add)
+            pv3 = v_u[s // 2][:, s % 2, :].rearrange("p (o m) -> p o m", m=3)
+            nc.vector.tensor_tensor(out=dg[:, 0:128], in0=pv3[:, :, 0], in1=pv3[:, :, 1], op=ALU.add)
 
-        def v_redt(s):
-            nc.vector.tensor_reduce(out=dg_t[s][:, 128:256],
-                                    in_=t_u[s // 2][:, s % 2, :].rearrange("p (o m) -> p o m", m=5),
-                                    axis=AX.X, op=ALU.add)
+        def v_sum_bc(s):
+            bc = work.tile([P, P, 2], F32, name="bc", tag="bc")
+            bc_t[s] = bc
+            pt5 = t_u[s // 2][:, s % 2, :].rearrange("p (o m) -> p o m", m=5)
+            nc.vector.tensor_tensor(out=bc[:], in0=pt5[:, :, 0:4:2], in1=pt5[:, :, 1:4:2], op=ALU.add)
+
+        def v_sum_v(s):
+            pv3 = v_u[s // 2][:, s % 2, :].rearrange("p (o m) -> p o m", m=3)
+            nc.vector.tensor_tensor(out=dg_t[s][:, 0:128], in0=dg_t[s][:, 0:128], in1=pv3[:, :, 2], op=ALU.add)
+
+        def v_sum_d(s):
+            nc.vector.tensor_tensor(out=dg_t[s][:, 128:256], in0=bc_t[s][:, :, 0], in1=bc_t[s][:, :, 1], op=ALU.add)
+
+        def v_sum_t(s):
+            pt5 = t_u[s // 2][:, s % 2, :].rearrange("p (o m) -> p o m", m=5)
+            nc.vector.tensor_tensor(out=dg_t[s][:, 128:256], in0=dg_t[s][:, 128:256], in1=pt5[:, :, 4], op=ALU.add)
 
         def v_dzg(s):
             nc.vector.scalar_tensor_tensor(out=dzn[:, s, 768:1024], in0=q_t[s][:], scalar=0.25,
@@ -319,7 +339,7 @@ def tile_equivariantmlpblock_v_kernel(tc, x, W0, W1, W2, s_out, v_out, t_out, gr
                                 start=(g == 0), stop=(g == 1))
 
         def dw_out(it0, h):
-            o1 = work.tile([P, 2, 512], F32, name="o1", tag="o1", bufs=3)
+            o1 = work.tile([P, 2, 512], F32, name="o1", tag="o1", bufs=3, align_bytes=64)
             evac(1, o1[:, 0, :], grp_t[(it0, h)][:], C768)
             evac(0, o1[:, 1, :], grp_t[(it0 + 1, h)][:], C768)
             nc.sync.dma_start(out=o1_v[:, it0:it0 + 2, 512 * h:512 * (h + 1)], in_=o1[:])
@@ -328,20 +348,11 @@ def tile_equivariantmlpblock_v_kernel(tc, x, W0, W1, W2, s_out, v_out, t_out, gr
             pw = psum.tile([P, P], BF16, name="pw12", tag=bank, bufs=(2 if bank == "pg" else 1))
             nc.tensor.transpose(pw[:], raw[:], ident_b[:])
             nc.scalar.copy(out=dst[:], in_=pw[:])
-        for c in range(3):
-            w0_turn(c)
-        x_copy(0)
-        x_copy(1)
-        for k in range(2, 6):
-            x_quant(k - 2)
-            x_copy(k)
-        x_quant(4)
-        x_quant(5)
-        for c in range(3):
-            w0_quant(c)
         p1(0)
         s1(0)
 
+        copies = {1: (("x", 0),), 2: (("x", 1),), 3: (("x", 2), ("x", 3)), 4: (("x", 4), ("dz", 0)),
+                  5: (("x", 5), ("dz", 1)), 6: (("dz", 2),)}
         early = ("pz", "pg", "pg")
         late = ("pB", "pA", "pd")
         for s in range(8):
@@ -353,32 +364,51 @@ def tile_equivariantmlpblock_v_kernel(tc, x, W0, W1, W2, s_out, v_out, t_out, gr
             v_ht(s)
             if s >= 1:
                 s4(s - 1)
-            if s < 7:
+            if 1 <= s < 7:
                 p1(s + 1)
                 s1(s + 1)
-            else:
+            if s == 7:
                 for it in range(3):
                     dw_pass(it, 0, 0, early[it])
             s2(s)
             p2(s)
+            if s == 0:
+                p1(1)
+                s1(1)
             v_prodv(s)
+            v_prodt(s)
             v_dzs(s)
             s3v(s)
             s3t(s)
-            v_prodt(s)
-            v_redv(s)
+            if s == 0:
+                for c in range(3):
+                    w0_turn(c)
+            v_sum_a(s)
+            v_sum_bc(s)
+            v_sum_v(s)
+            v_sum_d(s)
+            if s == 1:
+                for c in range(3):
+                    w0_quant(c)
+            for (what, c) in copies.get(s - 1, ()):
+                if what == "x":
+                    x_quant(c)
+                else:
+                    tok_quant(0, c)
             if s >= 1:
                 v3(s - 1)
                 p4(s - 1)
-            if s >= 5:
-                tok_quant(0, s - 5)
-            v_redt(s)
+            v_sum_t(s)
             if s >= 1:
                 s5(s - 1, 0)
             if s == 1 or s == 2:
-                load_rows(3, s - 1, s)
-            if 4 <= s <= 6:
-                tok_copy(0, s - 4, 0)
+                load_gz(s + 5)
+                load_vt(s + 5)
+            for (what, c) in copies.get(s, ()):
+                if what == "x":
+                    x_copy(c)
+                else:
+                    tok_copy(0, c, 0)
 
         v_dzg(7)
         p3(7)

@@ -154,7 +154,6 @@ def tile_equivariantmlpblock_v_kernel(tc, x, W0, W1, W2, s_out, v_out, t_out, gr
         tS_t = {}
         q_t = {}
         dg_t = {}
-        bc_t = {}
         pv_t = {}
         pd_t = {}
         dTg_t = {}
@@ -215,28 +214,16 @@ def tile_equivariantmlpblock_v_kernel(tc, x, W0, W1, W2, s_out, v_out, t_out, gr
             nc.vector.scalar_tensor_tensor(out=tt, in0=go_u[s // 2][:, s % 2, 1152:1792], scalar=-1.0, in1=tt,
                                            op0=ALU.mult, op1=ALU.mult)
 
-        def v_sum_a(s):
+        def v_redv(s):
             dg = work.tile([P, 256], F32, name="dg", tag="dg")
             dg_t[s] = dg
-            pv3 = v_u[s // 2][:, s % 2, :].rearrange("p (o m) -> p o m", m=3)
-            nc.vector.tensor_tensor(out=dg[:, 0:128], in0=pv3[:, :, 0], in1=pv3[:, :, 1], op=ALU.add)
+            nc.vector.tensor_reduce(out=dg[:, 0:128], in_=v_u[s // 2][:, s % 2, :].rearrange("p (o m) -> p o m", m=3),
+                                    axis=AX.X, op=ALU.add)
 
-        def v_sum_bc(s):
-            bc = work.tile([P, P, 2], F32, name="bc", tag="bc")
-            bc_t[s] = bc
-            pt5 = t_u[s // 2][:, s % 2, :].rearrange("p (o m) -> p o m", m=5)
-            nc.vector.tensor_tensor(out=bc[:], in0=pt5[:, :, 0:4:2], in1=pt5[:, :, 1:4:2], op=ALU.add)
-
-        def v_sum_v(s):
-            pv3 = v_u[s // 2][:, s % 2, :].rearrange("p (o m) -> p o m", m=3)
-            nc.vector.tensor_tensor(out=dg_t[s][:, 0:128], in0=dg_t[s][:, 0:128], in1=pv3[:, :, 2], op=ALU.add)
-
-        def v_sum_d(s):
-            nc.vector.tensor_tensor(out=dg_t[s][:, 128:256], in0=bc_t[s][:, :, 0], in1=bc_t[s][:, :, 1], op=ALU.add)
-
-        def v_sum_t(s):
-            pt5 = t_u[s // 2][:, s % 2, :].rearrange("p (o m) -> p o m", m=5)
-            nc.vector.tensor_tensor(out=dg_t[s][:, 128:256], in0=dg_t[s][:, 128:256], in1=pt5[:, :, 4], op=ALU.add)
+        def v_redt(s):
+            nc.vector.tensor_reduce(out=dg_t[s][:, 128:256],
+                                    in_=t_u[s // 2][:, s % 2, :].rearrange("p (o m) -> p o m", m=5),
+                                    axis=AX.X, op=ALU.add)
 
         def v_dzg(s):
             nc.vector.scalar_tensor_tensor(out=dzn[:, s, 768:1024], in0=q_t[s][:], scalar=0.25,
@@ -267,6 +254,7 @@ def tile_equivariantmlpblock_v_kernel(tc, x, W0, W1, W2, s_out, v_out, t_out, gr
             nc.gpsimd.tensor_scalar(out=o0_t[s][:, 1152:1792].rearrange("p (i m) -> p i m", m=5),
                                     in0=tS[:].rearrange("p m i -> p i m"),
                                     scalar1=1.0, scalar2=0.0, op0=ALU.mult, op1=ALU.add)
+            nc.sync.dma_start(out=o0_v[:, s // 4, s % 4, 768:1792], in_=o0_t[s][:, 768:1792])
 
         def p3(s):
             words = dzn[:, s, :].bitcast(F32)
@@ -308,7 +296,7 @@ def tile_equivariantmlpblock_v_kernel(tc, x, W0, W1, W2, s_out, v_out, t_out, gr
             o0 = o0_t[s]
             evac(0, o0[:, 0:512], pm_t[s][0][:], C768)
             evac(eng1, o0[:, 512:768], pm_t[s][1][:, 256:512], C768)
-            nc.sync.dma_start(out=o0_v[:, s // 4, s % 4, :], in_=o0[:])
+            nc.sync.dma_start(out=o0_v[:, s // 4, s % 4, 0:768], in_=o0[:, 0:768])
 
         dk_t = {}
 
@@ -376,17 +364,14 @@ def tile_equivariantmlpblock_v_kernel(tc, x, W0, W1, W2, s_out, v_out, t_out, gr
                 p1(1)
                 s1(1)
             v_prodv(s)
-            v_prodt(s)
             v_dzs(s)
             s3v(s)
             s3t(s)
             if s == 0:
                 for c in range(3):
                     w0_turn(c)
-            v_sum_a(s)
-            v_sum_bc(s)
-            v_sum_v(s)
-            v_sum_d(s)
+            v_prodt(s)
+            v_redv(s)
             if s == 1:
                 for c in range(3):
                     w0_quant(c)
@@ -398,7 +383,7 @@ def tile_equivariantmlpblock_v_kernel(tc, x, W0, W1, W2, s_out, v_out, t_out, gr
             if s >= 1:
                 v3(s - 1)
                 p4(s - 1)
-            v_sum_t(s)
+            v_redt(s)
             if s >= 1:
                 s5(s - 1, 0)
             if s == 1 or s == 2:

from contextlib import ExitStack
import math

import concourse.masks as masks
import concourse.mybir as mybir

FLOPS = 2 * 2 * 1024 * 1024 * 768 + 2 * 1024 * 8 * 128 * 128
BYTES = 25755648

F32 = mybir.dt.float32
BF16 = mybir.dt.bfloat16
U32 = mybir.dt.uint32
U8 = mybir.dt.uint8
E4 = mybir.dt.float8_e4m3fn_x4
E5 = mybir.dt.float8_e5m2_x4
ALU = mybir.AluOpType
ACT = mybir.ActivationFunctionType
AX = mybir.AxisListType

P = 128
C768 = 1.0 / math.sqrt(768.0)
C128 = 1.0 / math.sqrt(128.0)


def tile_equivariantmlpblock_v_kernel(tc, x, W0, W1, W2, s_out, v_out, t_out, grad_out, out_0, out_1):
    nc = tc.nc

    go_v = grad_out.rearrange("(g p j) w -> p g j w", g=2, j=4)
    z_v = s_out.rearrange("(g p j) w -> p g j w", g=2, j=4)
    v_v = v_out.rearrange("(g p j) o m -> p g j (o m)", g=2, j=4)
    t_v = t_out.rearrange("(g p j) o m -> p g j (o m)", g=2, j=4)
    x_v = x.rearrange("(g p j) w -> p g j w", g=2, j=4)
    w0_v = W0.rearrange("(t p) f -> p t f", p=P)
    o0_v = out_0.rearrange("(g p j) w -> p g j w", g=2, j=4)
    o1_v = out_1.rearrange("(t p) f -> p t f", p=P)

    with ExitStack() as ctx:
        const = ctx.enter_context(tc.tile_pool(name="const", bufs=1))
        inp = ctx.enter_context(tc.tile_pool(name="inp", bufs=1))
        work = ctx.enter_context(tc.tile_pool(name="work", bufs=2))
        psum = ctx.enter_context(tc.psum_pool(name="psum", bufs=1))
        ctx.enter_context(tc.manual_schedule())

        ident_f = const.tile([P, P], F32, name="ident_f")
        masks.make_identity(nc, ident_f[:])
        ident_b = const.tile([P, P], BF16, name="ident_b")
        masks.make_identity(nc, ident_b[:])
        neg_half = const.tile([P, 1], F32, name="neg_half")
        nc.vector.memset(neg_half[:], -0.5)
        warm = const.tile([P, 1], F32, name="warm")
        nc.scalar.activation(out=warm[:], in_=neg_half[:], func=ACT.Sigmoid)

        w1_raw = inp.tile([P, P], BF16, name="w1_raw")
        nc.sync.dma_start(out=w1_raw[:], in_=W1)
        w2_raw = inp.tile([P, P], BF16, name="w2_raw")
        nc.sync.dma_start(out=w2_raw[:], in_=W2)
        x_raw = []
        for g in range(2):
            x_raw.append(inp.tile([P, 4, 768], BF16, name="x_raw%d" % g))
        go_u = []
        z_u = []
        v_u = []
        t_u = []
        for U in range(4):
            go_u.append(inp.tile([P, 2, 1792], BF16, name="go%d" % U))
            z_u.append(inp.tile([P, 2, 1024], F32, name="z%d" % U))
            v_u.append(inp.tile([P, 2, 384], F32, name="v%d" % U))
            t_u.append(inp.tile([P, 2, 640], F32, name="t%d" % U))
        w0_raw = inp.tile([P, 6, 1024], BF16, name="w0_raw")

        def load_x(g):
            nc.sync.dma_start(out=x_raw[g][:], in_=x_v[:, g, :, 0:768])

        def load_gz(s):
            nc.sync.dma_start(out=go_u[s // 2][:, s % 2, :], in_=go_v[:, s // 4, s % 4, :])
            nc.sync.dma_start(out=z_u[s // 2][:, s % 2, :], in_=z_v[:, s // 4, s % 4, :])

        def load_vt(s):
            nc.sync.dma_start(out=v_u[s // 2][:, s % 2, :], in_=v_v[:, s // 4, s % 4, :])
            nc.sync.dma_start(out=t_u[s // 2][:, s % 2, :], in_=t_v[:, s // 4, s % 4, :])

        load_gz(0)
        load_vt(0)
        load_gz(1)
        for c in range(3):
            nc.sync.dma_start(out=w0_raw[:, 2 * c:2 * c + 2, :], in_=w0_v[:, 2 * c:2 * c + 2, :])
        load_vt(1)
        for s in range(2, 6):
            load_gz(s)
            load_vt(s)
            if s % 2 == 0:
                load_x(s // 2 - 1)

        w0c = const.tile([P, 2, 768], U32, name="w0c", align_bytes=64)
        w0s = const.tile([P, 2, 768], U8, name="w0s", align_bytes=64)
        xc = const.tile([P, 2, 768], U32, name="xc", align_bytes=64)
        xs = const.tile([P, 2, 768], U8, name="xs", align_bytes=64)
        dkc = const.tile([P, 2, 1024], U32, name="dkc", align_bytes=64)
        dks = const.tile([P, 2, 1024], U8, name="dks", align_bytes=64)
        dzn = const.tile([P, 8, 1024], BF16, name="dzn", align_bytes=64)
        w1T = const.tile([P, P], F32, name="w1T")
        w2T = const.tile([P, P], F32, name="w2T")

        def evac(eng, out, in_, scale):
            if eng == 0:
                nc.scalar.activation(out=out, in_=in_, func=ACT.Copy, scale=scale)
            else:
                nc.vector.tensor_scalar(out=out, in0=in_, scalar1=scale, scalar2=None, op0=ALU.mult)

        xg_t = {}

        def x_copy(k):
            g = k // 3
            c = k % 3
            xg = work.tile([P, 256, 4], BF16, name="xg", tag="dk", bufs=4, align_bytes=64)
            nc.scalar.copy(out=xg[:], in_=x_raw[g][:, :, 256 * c:256 * (c + 1)].rearrange("p j i -> p i j"))
            xg_t[k] = xg

        def x_quant(k):
            g = k // 3
            c = k % 3
            nc.vector.quantize_mx(out=xc[:, g, 256 * c:256 * (c + 1)].bitcast(E4),
                                  scales=xs[:, g, 256 * c:256 * (c + 1)],
                                  in_=xg_t[k][:].rearrange("p i j -> p (i j)"))

        w0g_t = {}
        W0_BANKS = (("pm0", "pm1"), ("pd", "pm0"), ("pm1", "pd"))
        for c in range(3):
            w0g_t[c] = work.tile([P, 2, 256, 4], BF16, name="w0g%d" % c, tag="o1", bufs=3, align_bytes=64)

        def w0_turn(c):
            w0g = w0g_t[c]
            for s in range(2):
                words = w0_raw[:, 2 * c + s, :].bitcast(F32)
                pt = psum.tile([P, 2, 2, P], F32, name="pt", tag=W0_BANKS[c][s])
                for G in range(2):
                    for u in range(2):
                        nc.tensor.transpose(pt[:, G, u, :], words[:, 256 * G + u:256 * (G + 1):2], ident_f[:])
                for G in range(2):
                    nc.scalar.copy(out=w0g[:, G, P * s:P * (s + 1), :].bitcast(F32),
                                   in_=pt[:, G, :, :].rearrange("p u r -> p r u"))

        def w0_quant(c):
            for G in range(2):
                nc.vector.quantize_mx(out=w0c[:, G, 256 * c:256 * (c + 1)].bitcast(E4),
                                      scales=w0s[:, G, 256 * c:256 * (c + 1)],
                                      in_=w0g_t[c][:, G, :, :].rearrange("p i t -> p (i t)"))

        pz_t = {}
        pg_t = {}
        gT_t = {}
        hT_t = {}
        o0_t = {}
        tS_t = {}
        q_t = {}
        dg_t = {}
        pv_t = {}
        pd_t = {}
        dTg_t = {}
        dT_t = {}
        pm_t = {}

        def p1(s):
            go = go_u[s // 2]
            z = z_u[s // 2]
            e = s % 2
            pz = psum.tile([P, 2, P], F32, name="pz", tag="pz")
            for k in range(2):
                nc.tensor.transpose(pz[:, k, :], z[:, e, 768 + P * k:768 + P * (k + 1)], ident_f[:])
            pg = psum.tile([P, 8, P], BF16, name="pg", tag="pg", bufs=2)
            for m in range(3):
                nc.tensor.transpose(pg[:, m, :], go[:, e, 768 + m:1152:3], ident_b[:])
            for m in range(5):
                nc.tensor.transpose(pg[:, 3 + m, :], go[:, e, 1152 + m:1792:5], ident_b[:])
            pz_t[s] = pz
            pg_t[s] = pg

        def s1(s):
            gT = work.tile([P, 2, P], F32, name="gT", tag="gT")
            nc.scalar.activation(out=gT[:], in_=pz_t[s][:], func=ACT.Sigmoid)
            gT_t[s] = gT

        def s2(s):
            q = work.tile([P, 256], F32, name="q", tag="q")
            nc.scalar.activation(out=q[:], in_=z_u[s // 2][:, s % 2, 768:1024], func=ACT.Sigmoid)
            nc.scalar.activation(out=q[:], in_=q[:], func=ACT.Square, bias=neg_half[:])
            q_t[s] = q

        def v_mask(s):
            zs = z_u[s // 2][:, s % 2, 0:768]
            nc.vector.tensor_scalar(out=zs, in0=zs, scalar1=0.0, scalar2=0.01, op0=ALU.is_ge, op1=ALU.max)

        def v_dzs(s):
            nc.vector.tensor_tensor(out=dzn[:, s, 0:768], in0=go_u[s // 2][:, s % 2, 0:768],
                                    in1=z_u[s // 2][:, s % 2, 0:768], op=ALU.mult)

        def v_hv(s):
            hT = work.tile([P, 8, P], F32, name="hT", tag="hT")
            hT_t[s] = hT
            nc.vector.tensor_tensor(out=hT[:, 0:3, :], in0=pg_t[s][:, 0:3, :],
                                    in1=gT_t[s][:, 0:1, :].to_broadcast([P, 3, P]), op=ALU.mult)

        def v_ht(s):
            nc.vector.tensor_tensor(out=hT_t[s][:, 3:8, :], in0=pg_t[s][:, 3:8, :],
                                    in1=gT_t[s][:, 1:2, :].to_broadcast([P, 5, P]), op=ALU.mult)

        def v_prodv(s):
            vv = v_u[s // 2][:, s % 2, :]
            nc.vector.scalar_tensor_tensor(out=vv, in0=go_u[s // 2][:, s % 2, 768:1152], scalar=-1.0, in1=vv,
                                           op0=ALU.mult, op1=ALU.mult)

        def v_prodt(s):
            tt = t_u[s // 2][:, s % 2, :]
            nc.vector.scalar_tensor_tensor(out=tt, in0=go_u[s // 2][:, s % 2, 1152:1792], scalar=-1.0, in1=tt,
                                           op0=ALU.mult, op1=ALU.mult)

        def v_redv(s):
            dg = work.tile([P, 256], F32, name="dg", tag="dg")
            dg_t[s] = dg
            nc.vector.tensor_reduce(out=dg[:, 0:128], in_=v_u[s // 2][:, s % 2, :].rearrange("p (o m) -> p o m", m=3),
                                    axis=AX.X, op=ALU.add)

        def v_redt(s):
            nc.vector.tensor_reduce(out=dg_t[s][:, 128:256],
                                    in_=t_u[s // 2][:, s % 2, :].rearrange("p (o m) -> p o m", m=5),
                                    axis=AX.X, op=ALU.add)

        def v_dzg(s):
            nc.vector.scalar_tensor_tensor(out=dzn[:, s, 768:1024], in0=q_t[s][:], scalar=0.25,
                                           in1=dg_t[s][:], op0=ALU.subtract, op1=ALU.mult)

        def p2(s):
            pB = psum.tile([P, 4, P], F32, name="pB", tag="pB")
            for m in range(3):
                nc.tensor.matmul(pB[:, m, :], lhsT=hT_t[s][:, m, :], rhs=w1T[:], start=True, stop=True)
            nc.tensor.matmul(pB[:, 3, :], lhsT=hT_t[s][:, 7, :], rhs=w2T[:], start=True, stop=True)
            pA = psum.tile([P, 4, P], F32, name="pA", tag="pA")
            for m in range(4):
                nc.tensor.matmul(pA[:, m, :], lhsT=hT_t[s][:, 3 + m, :], rhs=w2T[:], start=True, stop=True)
            pv_t[s] = (pA, pB)

        def s3v(s):
            o0 = work.tile([P, 1792], F32, name="o0", tag="o0", bufs=4, align_bytes=64)
            o0_t[s] = o0
            tS = work.tile([P, 5, P], F32, name="tS", tag="tS")
            tS_t[s] = tS
            pB = pv_t[s][1]
            evac(0, o0[:, 768:1152].rearrange("p (i m) -> p i m", m=3), pB[:, 0:3, :].rearrange("p m i -> p i m"), C128)
            evac(0, tS[:, 4, :], pB[:, 3, :], C128)

        def s3t(s):
            tS = tS_t[s]
            evac(0, tS[:, 0:4, :], pv_t[s][0][:], C128)
            nc.gpsimd.tensor_scalar(out=o0_t[s][:, 1152:1792].rearrange("p (i m) -> p i m", m=5),
                                    in0=tS[:].rearrange("p m i -> p i m"),
                                    scalar1=1.0, scalar2=0.0, op0=ALU.mult, op1=ALU.add)
            nc.sync.dma_start(out=o0_v[:, s // 4, s % 4, 768:1792], in_=o0_t[s][:, 768:1792])

        def p3(s):
            words = dzn[:, s, :].bitcast(F32)
            pd = psum.tile([P, 2, 2, P], F32, name="pd", tag="pd")
            for G in range(2):
                for u in range(2):
                    nc.tensor.transpose(pd[:, G, u, :], words[:, 256 * G + u:256 * (G + 1):2], ident_f[:])
            pd_t[s] = pd

        def s4(s):
            dTg = work.tile([P, 2, P, 4], BF16, name="dTg", tag="dTg", align_bytes=64)
            for G in range(2):
                nc.scalar.copy(out=dTg[:, G, :, :].bitcast(F32), in_=pd_t[s][:, G, :, :].rearrange("p u r -> p r u"))
            dTg_t[s] = dTg

        def v3(s):
            dTc = work.tile([P, 256], U32, name="dTc", tag="dTc", align_bytes=64)
            dTs = work.tile([P, 256], U8, name="dTs", tag="dTs", align_bytes=64)
            nc.vector.quantize_mx(out=dTc[:].bitcast(E5), scales=dTs[:],
                                  in_=dTg_t[s][:].rearrange("p g r t -> p (g r t)"))
            dT_t[s] = (dTc, dTs)

        def p4(s):
            dTc, dTs = dT_t[s]
            pms = []
            for w in range(2):
                pm = psum.tile([P, 512], F32, name="pm", tag="pm%d" % w)
                for G in range(2):
                    nc.tensor.matmul_mx(out=pm[:],
                                        lhsT=dTc[:, P * G:P * (G + 1)].bitcast(E5),
                                        lhsT_scale=dTs[:, P * G:P * (G + 1)],
                                        rhs=w0c[:, G, 256 * w:256 * w + 512].bitcast(E4),
                                        rhs_scale=w0s[:, G, 256 * w:256 * w + 512],
                                        start=(G == 0), stop=(G == 1))
                pms.append(pm)
            pm_t[s] = pms

        def s5(s, eng1):
            o0 = o0_t[s]
            evac(0, o0[:, 0:512], pm_t[s][0][:], C768)
            evac(eng1, o0[:, 512:768], pm_t[s][1][:, 256:512], C768)
            nc.sync.dma_start(out=o0_v[:, s // 4, s % 4, 0:768], in_=o0[:, 0:768])

        dk_t = {}

        def tok_copy(g, c, eng):
            dk = work.tile([P, 256, 4], BF16, name="dk", tag="dk", bufs=4, align_bytes=64)
            src = dzn[:, 4 * g:4 * g + 4, 256 * c:256 * (c + 1)].rearrange("p j f -> p f j")
            if eng == 0:
                nc.scalar.copy(out=dk[:], in_=src)
            else:
                nc.vector.tensor_copy(out=dk[:], in_=src)
            dk_t[(g, c)] = dk

        def tok_quant(g, c):
            nc.vector.quantize_mx(out=dkc[:, g, 256 * c:256 * (c + 1)].bitcast(E5),
                                  scales=dks[:, g, 256 * c:256 * (c + 1)],
                                  in_=dk_t[(g, c)][:].rearrange("p f j -> p (f j)"))

        grp_t = {}

        def dw_pass(it, h, g, bank):
            if g == 0:
                grp_t[(it, h)] = psum.tile([P, 512], F32, name="pw", tag=bank, bufs=(2 if bank == "pg" else 1))
            nc.tensor.matmul_mx(out=grp_t[(it, h)][:],
                                lhsT=xc[:, g, P * it:P * (it + 1)].bitcast(E4),
                                lhsT_scale=xs[:, g, P * it:P * (it + 1)],
                                rhs=dkc[:, g, 512 * h:512 * (h + 1)].bitcast(E5),
                                rhs_scale=dks[:, g, 512 * h:512 * (h + 1)],
                                start=(g == 0), stop=(g == 1))

        def dw_out(it0, h):
            o1 = work.tile([P, 2, 512], F32, name="o1", tag="o1", bufs=3, align_bytes=64)
            evac(1, o1[:, 0, :], grp_t[(it0, h)][:], C768)
            evac(0, o1[:, 1, :], grp_t[(it0 + 1, h)][:], C768)
            nc.sync.dma_start(out=o1_v[:, it0:it0 + 2, 512 * h:512 * (h + 1)], in_=o1[:])

        for (raw, dst, bank) in ((w1_raw, w1T, "pg"), (w2_raw, w2T, "pz")):
            pw = psum.tile([P, P], BF16, name="pw12", tag=bank, bufs=(2 if bank == "pg" else 1))
            nc.tensor.transpose(pw[:], raw[:], ident_b[:])
            nc.scalar.copy(out=dst[:], in_=pw[:])
        p1(0)
        s1(0)

        copies = {1: (("x", 0),), 2: (("x", 1),), 3: (("x", 2), ("x", 3)), 4: (("x", 4), ("dz", 0)),
                  5: (("x", 5), ("dz", 1)), 6: (("dz", 2),)}
        early = ("pz", "pg", "pg")
        late = ("pB", "pA", "pd")
        for s in range(8):
            v_mask(s)
            if s >= 1:
                v_dzg(s - 1)
                p3(s - 1)
            v_hv(s)
            v_ht(s)
            if s >= 1:
                s4(s - 1)
            if 1 <= s < 7:
                p1(s + 1)
                s1(s + 1)
            if s == 7:
                for it in range(3):
                    dw_pass(it, 0, 0, early[it])
            s2(s)
            p2(s)
            if s == 0:
                p1(1)
                s1(1)
            v_prodv(s)
            v_dzs(s)
            s3v(s)
            s3t(s)
            if s == 0:
                for c in range(3):
                    w0_turn(c)
            v_prodt(s)
            v_redv(s)
            if s == 1:
                for c in range(3):
                    w0_quant(c)
            for (what, c) in copies.get(s - 1, ()):
                if what == "x":
                    x_quant(c)
                else:
                    tok_quant(0, c)
            if s >= 1:
                v3(s - 1)
                p4(s - 1)
            v_redt(s)
            if s >= 1:
                s5(s - 1, 0)
            if s == 1 or s == 2:
                load_gz(s + 5)
                load_vt(s + 5)
            for (what, c) in copies.get(s, ()):
                if what == "x":
                    x_copy(c)
                else:
                    tok_copy(0, c, 0)

        v_dzg(7)
        p3(7)
        tok_copy(1, 0, 1)
        tok_copy(1, 1, 1)
        s4(7)
        tok_copy(1, 3, 0)
        dw_pass(3, 0, 0, "pB")
        dw_pass(4, 0, 0, "pA")
        tok_quant(1, 0)
        tok_quant(1, 1)
        tok_copy(1, 2, 1)
        tok_copy(0, 3, 1)
        v3(7)
        for it in range(5):
            dw_pass(it, 0, 1, "")
        dw_pass(5, 0, 0, "pd")
        dw_pass(5, 0, 1, "")
        dw_out(0, 0)
        tok_quant(1, 2)
        tok_quant(0, 3)
        tok_quant(1, 3)
        dw_out(2, 0)
        dw_out(4, 0)
        p4(7)
        s5(7, 1)
        banks1 = early + late
        for it in range(6):
            dw_pass(it, 1, 0, banks1[it])
            dw_pass(it, 1, 1, "")
            if it % 2 == 1:
                dw_out(it - 1, 1)
